import numpy as np
import ml_dtypes


def mxq(x, axis, fmt="e4m3"):
    dtype, down = {"e4m3": (ml_dtypes.float8_e4m3fn, 7), "e5m2": (ml_dtypes.float8_e5m2, 14)}[fmt]
    v = np.moveaxis(np.asarray(x, np.float32).astype(ml_dtypes.bfloat16).astype(np.float64), axis, -1)
    blocks = v.reshape(v.shape[:-1] + (-1, 32))
    amax = np.abs(blocks).max(-1, keepdims=True)
    byte = np.maximum(np.where(amax > 0, np.frexp(amax)[1] - 1 + 127, 0) - down, 1)
    scale = np.exp2(byte - 127.0)
    codes = (blocks / scale).astype(np.float32).astype(dtype).astype(np.float64)
    return np.moveaxis((codes * scale).reshape(v.shape), -1, axis)


WIDE = False


def mx_kscale(k):
    if not WIDE:
        return np.ones(k)
    levels = np.array([10, -10, 5, -5, 0])
    a = np.random.permutation(np.resize(levels, k // 512 * 4)).reshape(k // 512, 4)
    idx = np.arange(k)
    return np.exp2(a[idx // 512, idx % 128 // 32])


BF16 = ml_dtypes.bfloat16


def bf(x):
    return np.asarray(x, np.float32).astype(BF16)


def f64(x):
    return np.asarray(x).astype(np.float64)


E2M1 = np.array([0.0, 0.5, 1.0, 1.5, 2.0, 3.0, 4.0, 6.0, -0.0, -0.5, -1.0, -1.5, -2.0, -3.0, -4.0, -6.0])


def pack_weight(w, fmt):
    k, n = w.shape
    w = f64(bf(w)).reshape(k // 32, 32, n)
    amax = np.abs(w).max(1)
    if fmt == "e4m3":
        byte = np.frexp(amax)[1] - 1 + 127 - 7
    else:
        mant, ex = np.frexp(amax / 6.0)
        byte = np.where(mant > 0.5, ex, ex - 1) + 127
    byte = np.clip(np.where(amax > 0, byte, 1), 1, 254)
    scaled = (w * np.exp2(127.0 - byte)[:, None, :]).reshape(k, n).astype(np.float32)
    by_word = np.ascontiguousarray(scaled.reshape(k // 512, 128, 4, n).transpose(0, 1, 3, 2))
    if fmt == "e4m3":
        words = by_word.astype(ml_dtypes.float8_e4m3fn).view(np.uint8)
    else:
        c = by_word.astype(ml_dtypes.float4_e2m1fn).view(np.uint8) & 0xF
        words = c[..., 0::2] | (c[..., 1::2] << 4)
    return np.ascontiguousarray(words), np.ascontiguousarray(byte.astype(np.uint8).reshape(k // 512, 16, n))


def unpack_weight(words, scales, fmt):
    g, p, n, _ = words.shape
    if fmt == "e4m3":
        vals = np.ascontiguousarray(words).view(ml_dtypes.float8_e4m3fn).astype(np.float64)
    else:
        nib = np.empty((g, p, n, 4), np.uint8)
        nib[..., 0::2] = words & 0xF
        nib[..., 1::2] = words >> 4
        vals = E2M1[nib]
    vals = vals * np.repeat(np.exp2(scales.astype(np.float64) - 127.0), 8, axis=1)[..., None]
    return vals.transpose(0, 1, 3, 2).reshape(g * 512, n)


B, H, W, C, I, O, NH = 1, 2, 256, 8192, 512, 512, 8
DH = I // NH
SCALE = DH ** -0.5
FMT = "e4m3"


def setup_inputs():
    s, t = mx_kscale(C), mx_kscale(I)
    sc = s[None, :, None, None]
    left_feat = bf(np.random.standard_normal((B, C, H, W)) * sc)
    right_feat = bf(np.random.standard_normal((B, C, H, W)) * sc)
    wq = np.random.standard_normal((I, C)) / np.sqrt(C) / s[None, :] * t[:, None]
    wk = np.random.standard_normal((I, C)) / np.sqrt(C) / s[None, :] / t[:, None]
    wq_words, wq_scales = pack_weight(np.ascontiguousarray(wq.T), FMT)
    wk_words, wk_scales = pack_weight(np.ascontiguousarray(wk.T), FMT)
    return {"left_feat": left_feat,
            "right_feat": right_feat,
            "wq_words": wq_words, "wq_scales": wq_scales,
            "wk_words": wk_words, "wk_scales": wk_scales}


def reference(left_feat, right_feat, wq_words, wq_scales, wk_words, wk_scales):
    lf = f64(left_feat).reshape(B, C, H * W)
    rf = f64(right_feat).reshape(B, C, H * W)
    q = unpack_weight(wq_words, wq_scales, FMT).T @ mxq(lf, 1, "e4m3")
    k = unpack_weight(wk_words, wk_scales, FMT).T @ mxq(rf, 1, "e4m3")
    q = q.reshape(B, I, H, W).transpose(0, 2, 3, 1)
    k = k.reshape(B, I, H, W).transpose(0, 2, 1, 3)
    return (mxq(q, 3, "e4m3") @ mxq(k, 2, "e4m3")) * SCALE

@@ -1,0 +1,160 @@
+import concourse.mybir as mybir
+
+FP8X4 = mybir.dt.float8_e4m3fn_x4
+BF16 = mybir.dt.bfloat16
+F32 = mybir.dt.float32
+I32 = mybir.dt.int32
+U32 = mybir.dt.uint32
+U8 = mybir.dt.uint8
+
+P = 128
+PACK = 4
+K_PASS = P * PACK
+C = 8192
+PASSES = C // K_PASS
+H = 2
+W = 256
+HW = H * W
+O = 512
+O_TILES = O // P
+W_TILES = W // P
+QUADRANTS = 4
+SHARED = 4
+LEAD = 2
+RUN = 4
+SCALE = 0.125
+
+FLOPS = 2 * 2 * O * C * HW + 2 * H * W * W * O
+
+
+def regroup(copy, grouped, rows):
+    copy(
+        out=grouped.rearrange("p (c i) t -> p c t i", i=RUN),
+        in_=rows.rearrange("p t (c i) -> p c t i", i=RUN),
+    )
+
+
+def tile_sttm_single_pa_k_kernel(
+    tc, left_feat, right_feat, wq_words, wq_scales, wk_words, wk_scales, out
+):
+    nc = tc.nc
+    sides = ("q", "k")
+    feature = {
+        "q": left_feat[0].rearrange("(g p t) h w -> p g t (h w)", p=P, t=PACK),
+        "k": right_feat[0].rearrange("(g p t) h w -> p g t (h w)", p=P, t=PACK),
+    }
+    words = {
+        "q": wq_words.rearrange("g p n t -> p g (n t)").bitcast(I32),
+        "k": wk_words.rearrange("g p n t -> p g (n t)").bitcast(I32),
+    }
+    scale_rows = {"q": wq_scales.bitcast(I32), "k": wk_scales.bitcast(I32)}
+    steps = [(side, g) for side in sides for g in range(PASSES)]
+
+    with (
+        tc.tile_pool(name="keep", bufs=1) as keep,
+        tc.tile_pool(name="raw", bufs=6) as raw_pool,
+        tc.tile_pool(name="stage", bufs=3) as stage,
+        tc.psum_pool(name="psum", bufs=8) as psum,
+    ):
+        w_codes = {}
+        w_planes = {}
+        codes = {}
+        planes = {}
+        for side in sides:
+            w_codes[side] = keep.tile([P, PASSES, O], U32, name="w_codes_" + side, align_bytes=64)
+            w_planes[side] = keep.tile(
+                [P, PASSES // SHARED, O], U8, name="w_planes_" + side, align_bytes=64
+            )
+            codes[side] = keep.tile([P, HW], U32, name="codes_" + side, align_bytes=64)
+            planes[side] = keep.tile([P, HW], U8, name="planes_" + side, align_bytes=64)
+            nc.vector.memset(w_planes[side][:].bitcast(I32), 0)
+
+        def load_feature(step):
+            side, g = steps[step]
+            raw = raw_pool.tile([P, PACK, HW], BF16, name="raw")
+            nc.sync.dma_start(out=raw[:], in_=feature[side][:, g])
+            return raw
+
+        def load_scale_planes(side, block):
+            passes = slice(SHARED * block, SHARED * (block + 1))
+            for quadrant in range(QUADRANTS):
+                nc.sync.dma_start(
+                    out=w_planes[side][32 * quadrant : 32 * quadrant + 16, block, :].bitcast(I32),
+                    in_=scale_rows[side][passes, 4 * quadrant : 4 * quadrant + 4, :],
+                )
+
+        def quantise_product(side, acc):
+            rounded = stage.tile([P, O_TILES, HW], BF16, name="rounded")
+            for m in range(O_TILES):
+                copy = nc.vector.tensor_copy if m % 2 == 0 else nc.scalar.copy
+                copy(out=rounded[:, m, :], in_=acc[m][:])
+            grouped = stage.tile([P, HW, PACK], BF16, name="grouped", align_bytes=64)
+            for h in range(H):
+                cols = slice(h * W, (h + 1) * W)
+                copy = nc.vector.tensor_copy if h == 0 else nc.scalar.copy
+                regroup(copy, grouped[:, cols, :], rounded[:, :, cols])
+            for h in range(H):
+                cols = slice(h * W, (h + 1) * W)
+                nc.vector.quantize_mx(
+                    out=codes[side][:, cols].bitcast(FP8X4),
+                    scales=planes[side][:, cols],
+                    in_=grouped[:, cols, :].rearrange("p x t -> p (x t)"),
+                )
+
+        raws = {}
+        for step in range(LEAD):
+            raws[step] = load_feature(step)
+
+        acc = []
+        for step, (side, g) in enumerate(steps):
+            if step + LEAD < len(steps):
+                raws[step + LEAD] = load_feature(step + LEAD)
+            if g % SHARED == 0:
+                load_scale_planes(side, g // SHARED)
+            nc.sync.dma_start(out=w_codes[side][:, g, :].bitcast(I32), in_=words[side][:, g, :])
+
+            grouped = stage.tile([P, HW, PACK], BF16, name="grouped", align_bytes=64)
+            copy = nc.vector.tensor_copy if g % 2 == 0 else nc.scalar.copy
+            regroup(copy, grouped[:], raws[step][:])
+            f_codes = stage.tile([P, HW], U32, name="f_codes", align_bytes=64)
+            f_planes = stage.tile([P, HW], U8, name="f_planes", align_bytes=64)
+            nc.vector.quantize_mx(
+                out=f_codes[:].bitcast(FP8X4),
+                scales=f_planes[:],
+                in_=grouped[:].rearrange("p x t -> p (x t)"),
+            )
+
+            if g == 0:
+                acc = [psum.tile([P, HW], F32, name="acc%d" % m, tag="bank") for m in range(O_TILES)]
+            block, j = divmod(g, SHARED)
+            for m in range(O_TILES):
+                o_cols = slice(m * P, (m + 1) * P)
+                nc.tensor.matmul_mx(
+                    out=acc[m][:],
+                    lhsT=w_codes[side][:, g, o_cols].bitcast(FP8X4),
+                    lhsT_scale=w_planes[side][4 * j : P, block, o_cols],
+                    rhs=f_codes[:].bitcast(FP8X4),
+                    rhs_scale=f_planes[:],
+                    start=(g == 0),
+                    stop=(g == PASSES - 1),
+                )
+            if g == PASSES - 1:
+                quantise_product(side, acc)
+
+        for h in range(H):
+            x_cols = slice(h * W, (h + 1) * W)
+            dots = psum.tile([P, W_TILES, W], F32, name="dots", tag="bank")
+            for i in range(W_TILES):
+                w_cols = slice(h * W + i * P, h * W + (i + 1) * P)
+                nc.tensor.matmul_mx(
+                    out=dots[:, i, :],
+                    lhsT=codes["q"][:, w_cols].bitcast(FP8X4),
+                    lhsT_scale=planes["q"][:, w_cols],
+                    rhs=codes["k"][:, x_cols].bitcast(FP8X4),
+                    rhs_scale=planes["k"][:, x_cols],
+                    start=True,
+                    stop=True,
+                )
+            result = stage.tile([P, W_TILES, W], F32, name="result")
+            nc.vector.tensor_scalar_mul(out=result[:], in0=dots[:], scalar1=SCALE)
+            nc.sync.dma_start(out=out[0, h].rearrange("(i p) x -> p i x", p=P), in_=result[:])

@@ -27,11 +27,13 @@ SCALE = 0.125
 FLOPS = 2 * 2 * O * C * HW + 2 * H * W * W * O
 
 
-def regroup(copy, grouped, rows):
-    copy(
-        out=grouped.rearrange("p (c i) t -> p c t i", i=RUN),
-        in_=rows.rearrange("p t (c i) -> p c t i", i=RUN),
-    )
+def regroup(nc, grouped, rows):
+    for h, copy in enumerate((nc.vector.tensor_copy, nc.scalar.copy)):
+        cols = slice(h * W, (h + 1) * W)
+        copy(
+            out=grouped[:, cols, :].rearrange("p (c i) t -> p c t i", i=RUN),
+            in_=rows[:, :, cols].rearrange("p t (c i) -> p c t i", i=RUN),
+        )
 
 
 def tile_sttm_single_pa_k_kernel(
@@ -52,9 +54,11 @@ def tile_sttm_single_pa_k_kernel(
 
     with (
         tc.tile_pool(name="keep", bufs=1) as keep,
-        tc.tile_pool(name="raw", bufs=6) as raw_pool,
-        tc.tile_pool(name="stage", bufs=3) as stage,
+        tc.tile_pool(name="raw", bufs=8) as raw_pool,
+        tc.tile_pool(name="stage", bufs=4) as stage,
+        tc.tile_pool(name="quantised", bufs=6) as quantised,
         tc.psum_pool(name="psum", bufs=8) as psum,
+        tc.manual_schedule(),
     ):
         w_codes = {}
         w_planes = {}
@@ -89,10 +93,7 @@ def tile_sttm_single_pa_k_kernel(
                 copy = nc.vector.tensor_copy if m % 2 == 0 else nc.scalar.copy
                 copy(out=rounded[:, m, :], in_=acc[m][:])
             grouped = stage.tile([P, HW, PACK], BF16, name="grouped", align_bytes=64)
-            for h in range(H):
-                cols = slice(h * W, (h + 1) * W)
-                copy = nc.vector.tensor_copy if h == 0 else nc.scalar.copy
-                regroup(copy, grouped[:, cols, :], rounded[:, :, cols])
+            regroup(nc, grouped, rounded)
             for h in range(H):
                 cols = slice(h * W, (h + 1) * W)
                 nc.vector.quantize_mx(
@@ -101,9 +102,15 @@ def tile_sttm_single_pa_k_kernel(
                     in_=grouped[:, cols, :].rearrange("p x t -> p (x t)"),
                 )
 
+        def regroup_feature(raw):
+            grouped = stage.tile([P, HW, PACK], BF16, name="grouped", align_bytes=64)
+            regroup(nc, grouped, raw)
+            return grouped
+
         raws = {}
         for step in range(LEAD):
             raws[step] = load_feature(step)
+        groupeds = {0: regroup_feature(raws[0])}
 
         acc = []
         for step, (side, g) in enumerate(steps):
@@ -113,15 +120,14 @@ def tile_sttm_single_pa_k_kernel(
                 load_scale_planes(side, g // SHARED)
             nc.sync.dma_start(out=w_codes[side][:, g, :].bitcast(I32), in_=words[side][:, g, :])
 
-            grouped = stage.tile([P, HW, PACK], BF16, name="grouped", align_bytes=64)
-            copy = nc.vector.tensor_copy if g % 2 == 0 else nc.scalar.copy
-            regroup(copy, grouped[:], raws[step][:])
-            f_codes = stage.tile([P, HW], U32, name="f_codes", align_bytes=64)
-            f_planes = stage.tile([P, HW], U8, name="f_planes", align_bytes=64)
+            if step + 1 < len(steps):
+                groupeds[step + 1] = regroup_feature(raws[step + 1])
+            f_codes = quantised.tile([P, HW], U32, name="f_codes", align_bytes=64)
+            f_planes = quantised.tile([P, HW], U8, name="f_planes", align_bytes=64)
             nc.vector.quantize_mx(
                 out=f_codes[:].bitcast(FP8X4),
                 scales=f_planes[:],
-                in_=grouped[:].rearrange("p x t -> p (x t)"),
+                in_=groupeds[step][:].rearrange("p x t -> p (x t)"),
             )
 
             if g == 0:

@@ -18,8 +18,8 @@ HW = H * W
 O = 512
 O_TILES = O // P
 W_TILES = W // P
-QUADRANTS = 4
-SHARED = 4
+QUADRANT = 32
+LIVE = 4
 LEAD = 2
 RUN = 4
 SCALE = 0.125
@@ -49,14 +49,17 @@ def tile_sttm_single_pa_k_kernel(
         "q": wq_words.rearrange("g p n t -> p g (n t)").bitcast(I32),
         "k": wk_words.rearrange("g p n t -> p g (n t)").bitcast(I32),
     }
-    scale_rows = {"q": wq_scales.bitcast(I32), "k": wk_scales.bitcast(I32)}
+    scale_rows = {
+        "q": wq_scales.bitcast(F32).rearrange("g (a r) n -> r a g n", r=LIVE),
+        "k": wk_scales.bitcast(F32).rearrange("g (a r) n -> r a g n", r=LIVE),
+    }
     steps = [(side, g) for side in sides for g in range(PASSES)]
 
     with (
         tc.tile_pool(name="keep", bufs=1) as keep,
         tc.tile_pool(name="raw", bufs=8) as raw_pool,
         tc.tile_pool(name="stage", bufs=4) as stage,
-        tc.tile_pool(name="quantised", bufs=6) as quantised,
+        tc.tile_pool(name="quantised", bufs=8) as quantised,
         tc.psum_pool(name="psum", bufs=8) as psum,
         tc.manual_schedule(),
     ):
@@ -66,26 +69,21 @@ def tile_sttm_single_pa_k_kernel(
         planes = {}
         for side in sides:
             w_codes[side] = keep.tile([P, PASSES, O], U32, name="w_codes_" + side, align_bytes=64)
-            w_planes[side] = keep.tile(
-                [P, PASSES // SHARED, O], U8, name="w_planes_" + side, align_bytes=64
-            )
+            w_planes[side] = keep.tile([P, PASSES, O], U8, name="w_planes_" + side, align_bytes=64)
             codes[side] = keep.tile([P, HW], U32, name="codes_" + side, align_bytes=64)
             planes[side] = keep.tile([P, HW], U8, name="planes_" + side, align_bytes=64)
             nc.vector.memset(w_planes[side][:].bitcast(I32), 0)
+        for side in sides:
+            for r in range(LIVE):
+                nc.gpsimd.dma_start(
+                    out=w_planes[side][r:P:QUADRANT].bitcast(F32), in_=scale_rows[side][r]
+                )
 
         def load_feature(step):
             side, g = steps[step]
             raw = raw_pool.tile([P, PACK, HW], BF16, name="raw")
             nc.sync.dma_start(out=raw[:], in_=feature[side][:, g])
             return raw
-
-        def load_scale_planes(side, block):
-            passes = slice(SHARED * block, SHARED * (block + 1))
-            for quadrant in range(QUADRANTS):
-                nc.sync.dma_start(
-                    out=w_planes[side][32 * quadrant : 32 * quadrant + 16, block, :].bitcast(I32),
-                    in_=scale_rows[side][passes, 4 * quadrant : 4 * quadrant + 4, :],
-                )
 
         def quantise_product(side, acc):
             rounded = stage.tile([P, O_TILES, HW], BF16, name="rounded")
@@ -116,8 +114,6 @@ def tile_sttm_single_pa_k_kernel(
         for step, (side, g) in enumerate(steps):
             if step + LEAD < len(steps):
                 raws[step + LEAD] = load_feature(step + LEAD)
-            if g % SHARED == 0:
-                load_scale_planes(side, g // SHARED)
             nc.sync.dma_start(out=w_codes[side][:, g, :].bitcast(I32), in_=words[side][:, g, :])
 
             if step + 1 < len(steps):
@@ -132,13 +128,12 @@ def tile_sttm_single_pa_k_kernel(
 
             if g == 0:
                 acc = [psum.tile([P, HW], F32, name="acc%d" % m, tag="bank") for m in range(O_TILES)]
-            block, j = divmod(g, SHARED)
             for m in range(O_TILES):
                 o_cols = slice(m * P, (m + 1) * P)
                 nc.tensor.matmul_mx(
                     out=acc[m][:],
                     lhsT=w_codes[side][:, g, o_cols].bitcast(FP8X4),
-                    lhsT_scale=w_planes[side][4 * j : P, block, o_cols],
+                    lhsT_scale=w_planes[side][:, g, o_cols],
                     rhs=f_codes[:].bitcast(FP8X4),
                     rhs_scale=f_planes[:],
                     start=(g == 0),

import concourse.mybir as mybir

FP8X4 = mybir.dt.float8_e4m3fn_x4
BF16 = mybir.dt.bfloat16
F32 = mybir.dt.float32
I32 = mybir.dt.int32
U32 = mybir.dt.uint32
U8 = mybir.dt.uint8

P = 128
PACK = 4
K_PASS = P * PACK
C = 8192
PASSES = C // K_PASS
H = 2
W = 256
HW = H * W
O = 512
O_TILES = O // P
W_TILES = W // P
QUADRANT = 32
LIVE = 4
LEAD = 2
RUN = 4
SCALE = 0.125

FLOPS = 2 * 2 * O * C * HW + 2 * H * W * W * O


def regroup(nc, grouped, rows):
    for h, copy in enumerate((nc.vector.tensor_copy, nc.scalar.copy)):
        cols = slice(h * W, (h + 1) * W)
        copy(
            out=grouped[:, cols, :].rearrange("p (c i) t -> p c t i", i=RUN),
            in_=rows[:, :, cols].rearrange("p t (c i) -> p c t i", i=RUN),
        )


def tile_sttm_single_pa_k_kernel(
    tc, left_feat, right_feat, wq_words, wq_scales, wk_words, wk_scales, out
):
    nc = tc.nc
    sides = ("q", "k")
    feature = {
        "q": left_feat[0].rearrange("(g p t) h w -> p g t (h w)", p=P, t=PACK),
        "k": right_feat[0].rearrange("(g p t) h w -> p g t (h w)", p=P, t=PACK),
    }
    words = {
        "q": wq_words.rearrange("g p n t -> p g (n t)").bitcast(I32),
        "k": wk_words.rearrange("g p n t -> p g (n t)").bitcast(I32),
    }
    scale_rows = {
        "q": wq_scales.bitcast(F32).rearrange("g (a r) n -> r a g n", r=LIVE),
        "k": wk_scales.bitcast(F32).rearrange("g (a r) n -> r a g n", r=LIVE),
    }
    steps = [(side, g) for side in sides for g in range(PASSES)]

    with (
        tc.tile_pool(name="keep", bufs=1) as keep,
        tc.tile_pool(name="raw", bufs=8) as raw_pool,
        tc.tile_pool(name="stage", bufs=4) as stage,
        tc.tile_pool(name="quantised", bufs=8) as quantised,
        tc.psum_pool(name="psum", bufs=8) as psum,
        tc.manual_schedule(),
    ):
        w_codes = {}
        w_planes = {}
        codes = {}
        planes = {}
        for side in sides:
            w_codes[side] = keep.tile([P, PASSES, O], U32, name="w_codes_" + side, align_bytes=64)
            w_planes[side] = keep.tile([P, PASSES, O], U8, name="w_planes_" + side, align_bytes=64)
            codes[side] = keep.tile([P, HW], U32, name="codes_" + side, align_bytes=64)
            planes[side] = keep.tile([P, HW], U8, name="planes_" + side, align_bytes=64)
            nc.vector.memset(w_planes[side][:].bitcast(I32), 0)
        for side in sides:
            for r in range(LIVE):
                nc.gpsimd.dma_start(
                    out=w_planes[side][r:P:QUADRANT].bitcast(F32), in_=scale_rows[side][r]
                )

        def load_feature(step):
            side, g = steps[step]
            raw = raw_pool.tile([P, PACK, HW], BF16, name="raw")
            nc.sync.dma_start(out=raw[:], in_=feature[side][:, g])
            return raw

        def quantise_product(side, acc):
            rounded = stage.tile([P, O_TILES, HW], BF16, name="rounded")
            for m in range(O_TILES):
                copy = nc.vector.tensor_copy if m % 2 == 0 else nc.scalar.copy
                copy(out=rounded[:, m, :], in_=acc[m][:])
            grouped = stage.tile([P, HW, PACK], BF16, name="grouped", align_bytes=64)
            regroup(nc, grouped, rounded)
            for h in range(H):
                cols = slice(h * W, (h + 1) * W)
                nc.vector.quantize_mx(
                    out=codes[side][:, cols].bitcast(FP8X4),
                    scales=planes[side][:, cols],
                    in_=grouped[:, cols, :].rearrange("p x t -> p (x t)"),
                )

        def regroup_feature(raw):
            grouped = stage.tile([P, HW, PACK], BF16, name="grouped", align_bytes=64)
            regroup(nc, grouped, raw)
            return grouped

        raws = {}
        for step in range(LEAD):
            raws[step] = load_feature(step)
        groupeds = {0: regroup_feature(raws[0])}

        acc = []
        for step, (side, g) in enumerate(steps):
            if step + LEAD < len(steps):
                raws[step + LEAD] = load_feature(step + LEAD)
            nc.sync.dma_start(out=w_codes[side][:, g, :].bitcast(I32), in_=words[side][:, g, :])

            if step + 1 < len(steps):
                groupeds[step + 1] = regroup_feature(raws[step + 1])
            f_codes = quantised.tile([P, HW], U32, name="f_codes", align_bytes=64)
            f_planes = quantised.tile([P, HW], U8, name="f_planes", align_bytes=64)
            nc.vector.quantize_mx(
                out=f_codes[:].bitcast(FP8X4),
                scales=f_planes[:],
                in_=groupeds[step][:].rearrange("p x t -> p (x t)"),
            )

            if g == 0:
                acc = [psum.tile([P, HW], F32, name="acc%d" % m, tag="bank") for m in range(O_TILES)]
            for m in range(O_TILES):
                o_cols = slice(m * P, (m + 1) * P)
                nc.tensor.matmul_mx(
                    out=acc[m][:],
                    lhsT=w_codes[side][:, g, o_cols].bitcast(FP8X4),
                    lhsT_scale=w_planes[side][:, g, o_cols],
                    rhs=f_codes[:].bitcast(FP8X4),
                    rhs_scale=f_planes[:],
                    start=(g == 0),
                    stop=(g == PASSES - 1),
                )
            if g == PASSES - 1:
                quantise_product(side, acc)

        for h in range(H):
            x_cols = slice(h * W, (h + 1) * W)
            dots = psum.tile([P, W_TILES, W], F32, name="dots", tag="bank")
            for i in range(W_TILES):
                w_cols = slice(h * W + i * P, h * W + (i + 1) * P)
                nc.tensor.matmul_mx(
                    out=dots[:, i, :],
                    lhsT=codes["q"][:, w_cols].bitcast(FP8X4),
                    lhsT_scale=planes["q"][:, w_cols],
                    rhs=codes["k"][:, x_cols].bitcast(FP8X4),
                    rhs_scale=planes["k"][:, x_cols],
                    start=True,
                    stop=True,
                )
            result = stage.tile([P, W_TILES, W], F32, name="result")
            nc.vector.tensor_scalar_mul(out=result[:], in0=dots[:], scalar1=SCALE)
            nc.sync.dma_start(out=out[0, h].rearrange("(i p) x -> p i x", p=P), in_=result[:])
